import numpy as np
import ml_dtypes


def mxq(x, axis, fmt="e4m3"):
    dtype, down = {"e4m3": (ml_dtypes.float8_e4m3fn, 7), "e5m2": (ml_dtypes.float8_e5m2, 14)}[fmt]
    v = np.moveaxis(np.asarray(x, np.float32).astype(ml_dtypes.bfloat16).astype(np.float64), axis, -1)
    blocks = v.reshape(v.shape[:-1] + (-1, 32))
    amax = np.abs(blocks).max(-1, keepdims=True)
    byte = np.maximum(np.where(amax > 0, np.frexp(amax)[1] - 1 + 127, 0) - down, 1)
    scale = np.exp2(byte - 127.0)
    codes = (blocks / scale).astype(np.float32).astype(dtype).astype(np.float64)
    return np.moveaxis((codes * scale).reshape(v.shape), -1, axis)


WIDE = False


def mx_kscale(k):
    if not WIDE:
        return np.ones(k)
    levels = np.array([10, -10, 5, -5, 0])
    a = np.random.permutation(np.resize(levels, k // 512 * 4)).reshape(k // 512, 4)
    idx = np.arange(k)
    return np.exp2(a[idx // 512, idx % 128 // 32])


BF16 = ml_dtypes.bfloat16


def bf(x):
    return np.asarray(x, np.float32).astype(BF16)


def f64(x):
    return np.asarray(x).astype(np.float64)


B, S, D_IN, D_OUT, R = 4, 1024, 512, 1024, 128
SCALING = 2.0


def setup_inputs():
    s = mx_kscale(D_IN)
    g = np.sqrt(np.mean(1.0 / (s * s)))
    return {"x": bf(np.random.standard_normal((B, S, D_IN)) * s),
            "weight": bf(np.random.standard_normal((D_OUT, D_IN)) / np.sqrt(D_IN) / s),
            "a_w": bf(np.random.standard_normal((R, D_IN)) / np.sqrt(D_IN) / s),
            "b_w": bf(np.random.standard_normal((D_OUT, R)) / np.sqrt(R)),
            "magnitude": bf((np.random.uniform(size=(1, D_OUT)) + 0.5) * g),
            "h_lora": bf(np.random.standard_normal((B, S, R)))}


def reference(x, weight, a_w, b_w, magnitude, h_lora):
    w = f64(weight)
    base_out = mxq(f64(x), 2, "e4m3") @ mxq(w, 1, "e4m3").T
    lora_out = SCALING * (f64(h_lora) @ f64(b_w).T)
    w_eff = w + SCALING * (f64(b_w) @ f64(a_w))
    weight_norm = np.sqrt((w_eff * w_eff).sum(axis=1))
    mag_norm_scale = (f64(magnitude) / weight_norm).reshape(1, 1, -1)
    dora_out = (mag_norm_scale - 1.0) * base_out + mag_norm_scale * lora_out
    return base_out + dora_out

@@ -1,0 +1,252 @@
+from contextlib import ExitStack
+
+import concourse.mybir as mybir
+from concourse.masks import make_identity
+
+F32 = mybir.dt.float32
+BF16 = mybir.dt.bfloat16
+U32 = mybir.dt.uint32
+U8 = mybir.dt.uint8
+FP8X4 = mybir.dt.float8_e4m3fn_x4
+ACT = mybir.ActivationFunctionType
+ALU = mybir.AluOpType
+
+P = 128
+TOKENS = 4096
+D_IN = 512
+D_OUT = 1024
+RANK = 128
+BANK = 512
+WORDS = D_IN // 2
+TOKEN_TILES = TOKENS // P
+OUT_TILES = D_OUT // P
+LOAD_TILES = 4
+PAIRS = TOKEN_TILES // 2
+AHEAD = 2
+LAG = 2
+HALVES = D_OUT // BANK
+
+FLOPS = 2 * TOKENS * D_OUT * (D_IN + RANK) + 2 * D_OUT * RANK * D_IN
+
+
+def tile_loralinear_pa_t_kernel(tc, x, weight, a_w, b_w, magnitude, h_lora, out):
+    nc = tc.nc
+    x_rows = x.flatten_outer_dims().rearrange("(p j) k -> p (j k)", j=TOKEN_TILES)
+    h_rows = h_lora.flatten_outer_dims().rearrange("(p j) r -> p (j r)", j=TOKEN_TILES)
+    out_rows = out.flatten_outer_dims().rearrange("(p j) o -> p j o", j=TOKEN_TILES)
+
+    with ExitStack() as stack:
+        keep = stack.enter_context(tc.tile_pool(name="keep", bufs=1))
+        work = stack.enter_context(tc.tile_pool(name="work", bufs=2))
+        psum = stack.enter_context(tc.psum_pool(name="psum", bufs=2))
+        stack.enter_context(tc.manual_schedule())
+
+        ident_bf16 = keep.tile([P, P], BF16)
+        make_identity(nc, ident_bf16[:])
+        ident_f32 = keep.tile([P, P], F32)
+        make_identity(nc, ident_f32[:])
+        one = keep.tile([P, 1], F32)
+        nc.vector.memset(one[:], 1.0)
+        nc.scalar.sqrt(one[:], one[:])
+
+        w_sb = keep.tile([P, OUT_TILES * D_IN], BF16)
+        x_sb = keep.tile([P, TOKEN_TILES * D_IN], BF16)
+        h_sb = keep.tile([P, TOKEN_TILES * RANK], BF16)
+        bw_sb = keep.tile([P, OUT_TILES * RANK], BF16)
+        aw_sb = keep.tile([P, D_IN], BF16)
+        mag_rows = keep.tile([P, P], BF16)
+        nc.vector.memset(mag_rows[:], 0.0)
+
+        def load_weight_half(half):
+            tiles = OUT_TILES // 2
+            nc.sync.dma_start(
+                out=w_sb[:, half * tiles * D_IN : (half + 1) * tiles * D_IN].rearrange(
+                    "p (a k) -> p a k", a=tiles
+                ),
+                in_=weight[half * tiles * P : (half + 1) * tiles * P, :].rearrange(
+                    "(a p) k -> p a k", p=P
+                ),
+            )
+
+        def load_x(c):
+            cols = slice(c * LOAD_TILES * D_IN, (c + 1) * LOAD_TILES * D_IN)
+            nc.sync.dma_start(out=x_sb[:, cols], in_=x_rows[:, cols])
+
+        def load_h_half(half):
+            cols = slice(half * TOKEN_TILES // 2 * RANK, (half + 1) * TOKEN_TILES // 2 * RANK)
+            nc.sync.dma_start(out=h_sb[:, cols], in_=h_rows[:, cols])
+
+        nc.sync.dma_start(
+            out=bw_sb[:].rearrange("p (a r) -> p a r", a=OUT_TILES),
+            in_=b_w.rearrange("(a p) r -> p a r", p=P),
+        )
+        nc.sync.dma_start(
+            out=mag_rows[0:OUT_TILES, :], in_=magnitude.rearrange("u (a p) -> (u a) p", p=P)
+        )
+        load_weight_half(0)
+        nc.sync.dma_start(out=aw_sb[:], in_=a_w)
+        load_weight_half(1)
+        load_x(0)
+        load_h_half(0)
+        load_x(1)
+        load_x(2)
+        load_h_half(1)
+        for c in range(3, TOKEN_TILES // LOAD_TILES):
+            load_x(c)
+
+        def regroup_two_row_tiles(words, first_tile, grouped_words, copy):
+            bank = psum.tile([P, 2, 2, P], F32, tag="tr", name="bank")
+            for i in range(2):
+                for u in range(2):
+                    first = (first_tile + i) * WORDS + u * P
+                    nc.tensor.transpose(bank[:, i, u, :], words[:, first : first + P], ident_f32[:])
+            copy(
+                out=grouped_words.rearrange("p (i r u) -> p i r u", i=2, u=2),
+                in_=bank[:].rearrange("p i u r -> p i r u"),
+            )
+
+        w_codes = keep.tile([P, D_OUT], U32, align_bytes=64)
+        w_scales = keep.tile([P, D_OUT], U8, align_bytes=64)
+        w_grouped = keep.tile([P, D_OUT * 4], BF16, align_bytes=64)
+        x_codes = keep.tile([P, TOKENS], U32, align_bytes=64)
+        x_scales = keep.tile([P, TOKENS], U8, align_bytes=64)
+        hT = keep.tile([P, TOKENS], BF16)
+        x_grouped = {}
+
+        def prepare_token_pair(q, copy):
+            x_grouped[q] = work.tile([P, 2 * P * 4], BF16, align_bytes=64, tag="xg", name="x_grouped")
+            regroup_two_row_tiles(x_sb[:].bitcast(F32), 2 * q, x_grouped[q][:].bitcast(F32), copy)
+            h_bank = psum.tile([P, 2 * P], BF16, tag="tr", name="h_bank")
+            for i in range(2):
+                j = 2 * q + i
+                nc.tensor.transpose(
+                    h_bank[:, i * P : (i + 1) * P], h_sb[:, j * RANK : (j + 1) * RANK], ident_bf16[:]
+                )
+            copy(out=hT[:, 2 * q * P : (2 * q + 2) * P], in_=h_bank[:])
+
+        def quantise_token_pair(q):
+            cols = slice(2 * q * P, (2 * q + 2) * P)
+            nc.vector.quantize_mx(
+                out=x_codes[:, cols].bitcast(FP8X4), scales=x_scales[:, cols], in_=x_grouped[q][:]
+            )
+
+        bw_bank = psum.tile([P, D_OUT], BF16, tag="tr", name="bw_bank")
+        for a in range(OUT_TILES):
+            nc.tensor.transpose(
+                bw_bank[:, a * P : (a + 1) * P], bw_sb[:, a * RANK : (a + 1) * RANK], ident_bf16[:]
+            )
+        bwT2 = keep.tile([P, D_OUT], BF16)
+        nc.scalar.mul(out=bwT2[:], in_=bw_bank[:], mul=2.0)
+        mag_bank = psum.tile([P, P], BF16, tag="tr", name="mag_bank")
+        nc.tensor.transpose(mag_bank[:], mag_rows[:], ident_bf16[:])
+        mag_col = keep.tile([P, OUT_TILES], F32)
+        nc.vector.tensor_copy(out=mag_col[:], in_=mag_bank[:, 0:OUT_TILES])
+
+        norm_sq = keep.tile([P, OUT_TILES], F32)
+        for pair in range(OUT_TILES // 2):
+            regroup_two_row_tiles(
+                w_sb[:].bitcast(F32),
+                2 * pair,
+                w_grouped[:].bitcast(F32)[:, pair * BANK : (pair + 1) * BANK],
+                nc.vector.tensor_copy,
+            )
+            for a in (2 * pair, 2 * pair + 1):
+                w_eff = psum.tile([P, D_IN], F32, tag="wm", name="w_eff")
+                nc.tensor.matmul(
+                    w_eff[:], lhsT=bwT2[:, a * P : (a + 1) * P], rhs=aw_sb[:], start=True, stop=False
+                )
+                nc.tensor.matmul(
+                    w_eff[:],
+                    lhsT=ident_bf16[:],
+                    rhs=w_sb[:, a * D_IN : (a + 1) * D_IN],
+                    start=False,
+                    stop=True,
+                )
+                squares = work.tile([P, D_IN], F32, tag="sq", name="squares")
+                nc.scalar.activation(
+                    out=squares[:], in_=w_eff[:], func=ACT.Square, accum_out=norm_sq[:, a : a + 1]
+                )
+            if pair >= OUT_TILES // 2 - AHEAD:
+                prepare_token_pair(pair - (OUT_TILES // 2 - AHEAD), nc.vector.tensor_copy)
+            if pair % 2 == 1:
+                half = pair // 2
+                nc.vector.quantize_mx(
+                    out=w_codes[:, half * BANK : (half + 1) * BANK].bitcast(FP8X4),
+                    scales=w_scales[:, half * BANK : (half + 1) * BANK],
+                    in_=w_grouped[:, half * BANK * 4 : (half + 1) * BANK * 4],
+                )
+        for q in range(AHEAD):
+            quantise_token_pair(q)
+
+        norm = keep.tile([P, OUT_TILES], F32)
+        nc.scalar.sqrt(norm[:], norm_sq[:])
+        m_col = keep.tile([P, OUT_TILES], F32)
+        nc.vector.reciprocal(m_col[:], norm[:])
+        nc.vector.tensor_tensor(out=m_col[:], in0=m_col[:], in1=mag_col[:], op=ALU.mult)
+        m_rep = keep.tile([P, D_OUT], F32)
+        nc.vector.tensor_copy(
+            out=m_rep[:].rearrange("p (a t) -> p a t", a=OUT_TILES),
+            in_=m_col[:].unsqueeze(2).to_broadcast([P, OUT_TILES, P]),
+        )
+        m_sb = keep.tile([P, D_OUT], F32)
+        m_banks = []
+
+        def spread_m():
+            for n in range(HALVES):
+                m_bank = psum.tile([P, BANK], F32, tag="wm", name="m_bank")
+                for i in range(BANK // P):
+                    a = n * (BANK // P) + i
+                    nc.tensor.transpose(
+                        m_bank[:, i * P : (i + 1) * P], m_rep[:, a * P : (a + 1) * P], ident_f32[:]
+                    )
+                nc.scalar.copy(out=m_sb[:, n * BANK : (n + 1) * BANK], in_=m_bank[:])
+                m_banks.append(m_bank)
+
+        results = {}
+
+        def sum_tile(j):
+            rows = slice(j * P, (j + 1) * P)
+            results[j] = work.tile([P, D_OUT], F32, tag="res", name="result", bufs=8)
+            for n in range(HALVES):
+                cols = slice(n * BANK, (n + 1) * BANK)
+                lora = psum.tile([P, BANK], F32, tag="lora", name="lora")
+                nc.tensor.matmul(lora[:], lhsT=hT[:, rows], rhs=bwT2[:, cols], start=True, stop=True)
+                base = psum.tile([P, BANK], F32, tag="base", name="base")
+                nc.tensor.matmul_mx(
+                    out=base[:],
+                    lhsT=x_codes[:, rows].bitcast(FP8X4),
+                    lhsT_scale=x_scales[:, rows],
+                    rhs=w_codes[:, cols].bitcast(FP8X4),
+                    rhs_scale=w_scales[:, cols],
+                    start=True,
+                    stop=True,
+                )
+                lora_sb = work.tile([P, BANK], F32, tag="lsb", name="lora_sb", bufs=4)
+                nc.scalar.copy(out=lora_sb[:], in_=lora[:])
+                nc.vector.tensor_tensor(out=results[j][:, cols], in0=base[:], in1=lora_sb[:], op=ALU.add)
+
+        def scale_and_store(j):
+            result = results[j]
+            if j % 3 == 1:
+                for n in range(HALVES):
+                    cols = slice(n * BANK, (n + 1) * BANK)
+                    nc.vector.tensor_tensor(
+                        out=result[:, cols], in0=result[:, cols], in1=m_banks[n][:], op=ALU.mult
+                    )
+            else:
+                nc.gpsimd.tensor_tensor(out=result[:], in0=result[:], in1=m_sb[:], op=ALU.mult)
+            nc.sync.dma_start(out=out_rows[:, j, :], in_=result[:])
+
+        for j in range(TOKEN_TILES + LAG):
+            if j < TOKEN_TILES:
+                q_next = j // 2 + AHEAD
+                prepares = j % 2 == 0 and q_next < PAIRS
+                if prepares:
+                    prepare_token_pair(q_next, nc.scalar.copy)
+                sum_tile(j)
+                if prepares:
+                    quantise_token_pair(q_next)
+            if j == LAG - 1:
+                spread_m()
+            if j >= LAG:
+                scale_and_store(j - LAG)

@@ -38,7 +38,7 @@ def tile_loralinear_pa_t_kernel(tc, x, weight, a_w, b_w, magnitude, h_lora, out)
     with ExitStack() as stack:
         keep = stack.enter_context(tc.tile_pool(name="keep", bufs=1))
         work = stack.enter_context(tc.tile_pool(name="work", bufs=2))
-        psum = stack.enter_context(tc.psum_pool(name="psum", bufs=2))
+        psum = stack.enter_context(tc.psum_pool(name="psum", bufs=6))
         stack.enter_context(tc.manual_schedule())
 
         ident_bf16 = keep.tile([P, P], BF16)
@@ -95,7 +95,7 @@ def tile_loralinear_pa_t_kernel(tc, x, weight, a_w, b_w, magnitude, h_lora, out)
             load_x(c)
 
         def regroup_two_row_tiles(words, first_tile, grouped_words, copy):
-            bank = psum.tile([P, 2, 2, P], F32, tag="tr", name="bank")
+            bank = psum.tile([P, 2, 2, P], F32, tag="ring", name="bank")
             for i in range(2):
                 for u in range(2):
                     first = (first_tile + i) * WORDS + u * P
@@ -116,7 +116,7 @@ def tile_loralinear_pa_t_kernel(tc, x, weight, a_w, b_w, magnitude, h_lora, out)
         def prepare_token_pair(q, copy):
             x_grouped[q] = work.tile([P, 2 * P * 4], BF16, align_bytes=64, tag="xg", name="x_grouped")
             regroup_two_row_tiles(x_sb[:].bitcast(F32), 2 * q, x_grouped[q][:].bitcast(F32), copy)
-            h_bank = psum.tile([P, 2 * P], BF16, tag="tr", name="h_bank")
+            h_bank = psum.tile([P, 2 * P], BF16, tag="ring", name="h_bank")
             for i in range(2):
                 j = 2 * q + i
                 nc.tensor.transpose(
@@ -130,14 +130,14 @@ def tile_loralinear_pa_t_kernel(tc, x, weight, a_w, b_w, magnitude, h_lora, out)
                 out=x_codes[:, cols].bitcast(FP8X4), scales=x_scales[:, cols], in_=x_grouped[q][:]
             )
 
-        bw_bank = psum.tile([P, D_OUT], BF16, tag="tr", name="bw_bank")
+        bw_bank = psum.tile([P, D_OUT], BF16, tag="ring", name="bw_bank")
         for a in range(OUT_TILES):
             nc.tensor.transpose(
                 bw_bank[:, a * P : (a + 1) * P], bw_sb[:, a * RANK : (a + 1) * RANK], ident_bf16[:]
             )
         bwT2 = keep.tile([P, D_OUT], BF16)
         nc.scalar.mul(out=bwT2[:], in_=bw_bank[:], mul=2.0)
-        mag_bank = psum.tile([P, P], BF16, tag="tr", name="mag_bank")
+        mag_bank = psum.tile([P, P], BF16, tag="ring", name="mag_bank")
         nc.tensor.transpose(mag_bank[:], mag_rows[:], ident_bf16[:])
         mag_col = keep.tile([P, OUT_TILES], F32)
         nc.vector.tensor_copy(out=mag_col[:], in_=mag_bank[:, 0:OUT_TILES])
@@ -151,7 +151,7 @@ def tile_loralinear_pa_t_kernel(tc, x, weight, a_w, b_w, magnitude, h_lora, out)
                 nc.vector.tensor_copy,
             )
             for a in (2 * pair, 2 * pair + 1):
-                w_eff = psum.tile([P, D_IN], F32, tag="wm", name="w_eff")
+                w_eff = psum.tile([P, D_IN], F32, tag="ring", name="w_eff")
                 nc.tensor.matmul(
                     w_eff[:], lhsT=bwT2[:, a * P : (a + 1) * P], rhs=aw_sb[:], start=True, stop=False
                 )
@@ -193,7 +193,7 @@ def tile_loralinear_pa_t_kernel(tc, x, weight, a_w, b_w, magnitude, h_lora, out)
 
         def spread_m():
             for n in range(HALVES):
-                m_bank = psum.tile([P, BANK], F32, tag="wm", name="m_bank")
+                m_bank = psum.tile([P, BANK], F32, tag="m", name="m_bank", bufs=HALVES)
                 for i in range(BANK // P):
                     a = n * (BANK // P) + i
                     nc.tensor.transpose(
@@ -204,14 +204,23 @@ def tile_loralinear_pa_t_kernel(tc, x, weight, a_w, b_w, magnitude, h_lora, out)
 
         results = {}
 
+        lora_sb = {}
+
+        def adapter_tile(j):
+            rows = slice(j * P, (j + 1) * P)
+            for n in range(HALVES):
+                cols = slice(n * BANK, (n + 1) * BANK)
+                lora = psum.tile([P, BANK], F32, tag="ring", name="lora")
+                nc.tensor.matmul(lora[:], lhsT=hT[:, rows], rhs=bwT2[:, cols], start=True, stop=True)
+                lora_sb[j, n] = work.tile([P, BANK], F32, tag="lsb", name="lora_sb", bufs=6)
+                nc.scalar.copy(out=lora_sb[j, n][:], in_=lora[:])
+
         def sum_tile(j):
             rows = slice(j * P, (j + 1) * P)
             results[j] = work.tile([P, D_OUT], F32, tag="res", name="result", bufs=8)
             for n in range(HALVES):
                 cols = slice(n * BANK, (n + 1) * BANK)
-                lora = psum.tile([P, BANK], F32, tag="lora", name="lora")
-                nc.tensor.matmul(lora[:], lhsT=hT[:, rows], rhs=bwT2[:, cols], start=True, stop=True)
-                base = psum.tile([P, BANK], F32, tag="base", name="base")
+                base = psum.tile([P, BANK], F32, tag="ring", name="base")
                 nc.tensor.matmul_mx(
                     out=base[:],
                     lhsT=x_codes[:, rows].bitcast(FP8X4),
@@ -221,9 +230,9 @@ def tile_loralinear_pa_t_kernel(tc, x, weight, a_w, b_w, magnitude, h_lora, out)
                     start=True,
                     stop=True,
                 )
-                lora_sb = work.tile([P, BANK], F32, tag="lsb", name="lora_sb", bufs=4)
-                nc.scalar.copy(out=lora_sb[:], in_=lora[:])
-                nc.vector.tensor_tensor(out=results[j][:, cols], in0=base[:], in1=lora_sb[:], op=ALU.add)
+                nc.vector.tensor_tensor(
+                    out=results[j][:, cols], in0=base[:], in1=lora_sb[j, n][:], op=ALU.add
+                )
 
         def scale_and_store(j):
             result = results[j]
@@ -237,12 +246,15 @@ def tile_loralinear_pa_t_kernel(tc, x, weight, a_w, b_w, magnitude, h_lora, out)
                 nc.gpsimd.tensor_tensor(out=result[:], in0=result[:], in1=m_sb[:], op=ALU.mult)
             nc.sync.dma_start(out=out_rows[:, j, :], in_=result[:])
 
+        adapter_tile(0)
         for j in range(TOKEN_TILES + LAG):
             if j < TOKEN_TILES:
                 q_next = j // 2 + AHEAD
                 prepares = j % 2 == 0 and q_next < PAIRS
                 if prepares:
                     prepare_token_pair(q_next, nc.scalar.copy)
+                if j + 1 < TOKEN_TILES:
+                    adapter_tile(j + 1)
                 sum_tile(j)
                 if prepares:
                     quantise_token_pair(q_next)

@@ -236,7 +236,7 @@ def tile_loralinear_pa_t_kernel(tc, x, weight, a_w, b_w, magnitude, h_lora, out)
 
         def scale_and_store(j):
             result = results[j]
-            if j % 3 == 1:
+            if j % 2 == 1:
                 for n in range(HALVES):
                     cols = slice(n * BANK, (n + 1) * BANK)
                     nc.vector.tensor_tensor(

@@ -38,7 +38,7 @@ def tile_loralinear_pa_t_kernel(tc, x, weight, a_w, b_w, magnitude, h_lora, out)
     with ExitStack() as stack:
         keep = stack.enter_context(tc.tile_pool(name="keep", bufs=1))
         work = stack.enter_context(tc.tile_pool(name="work", bufs=2))
-        psum = stack.enter_context(tc.psum_pool(name="psum", bufs=6))
+        psum = stack.enter_context(tc.psum_pool(name="psum", bufs=7))
         stack.enter_context(tc.manual_schedule())
 
         ident_bf16 = keep.tile([P, P], BF16)
@@ -188,19 +188,18 @@ def tile_loralinear_pa_t_kernel(tc, x, weight, a_w, b_w, magnitude, h_lora, out)
             out=m_rep[:].rearrange("p (a t) -> p a t", a=OUT_TILES),
             in_=m_col[:].unsqueeze(2).to_broadcast([P, OUT_TILES, P]),
         )
-        m_sb = keep.tile([P, D_OUT], F32)
-        m_banks = []
+        m_left = psum.tile([P, BANK], F32, tag="m", bufs=1)
+        m_right = keep.tile([P, BANK], F32)
 
         def spread_m():
-            for n in range(HALVES):
-                m_bank = psum.tile([P, BANK], F32, tag="m", name="m_bank", bufs=HALVES)
+            m_right_bank = psum.tile([P, BANK], F32, tag="ring")
+            for n, m_bank in enumerate((m_left, m_right_bank)):
                 for i in range(BANK // P):
                     a = n * (BANK // P) + i
                     nc.tensor.transpose(
                         m_bank[:, i * P : (i + 1) * P], m_rep[:, a * P : (a + 1) * P], ident_f32[:]
                     )
-                nc.scalar.copy(out=m_sb[:, n * BANK : (n + 1) * BANK], in_=m_bank[:])
-                m_banks.append(m_bank)
+            nc.scalar.copy(out=m_right[:], in_=m_right_bank[:])
 
         results = {}
 
@@ -236,14 +235,12 @@ def tile_loralinear_pa_t_kernel(tc, x, weight, a_w, b_w, magnitude, h_lora, out)
 
         def scale_and_store(j):
             result = results[j]
-            if j % 2 == 1:
-                for n in range(HALVES):
-                    cols = slice(n * BANK, (n + 1) * BANK)
-                    nc.vector.tensor_tensor(
-                        out=result[:, cols], in0=result[:, cols], in1=m_banks[n][:], op=ALU.mult
-                    )
-            else:
-                nc.gpsimd.tensor_tensor(out=result[:], in0=result[:], in1=m_sb[:], op=ALU.mult)
+            nc.vector.tensor_tensor(
+                out=result[:, 0:BANK], in0=result[:, 0:BANK], in1=m_left[:], op=ALU.mult
+            )
+            nc.gpsimd.tensor_tensor(
+                out=result[:, BANK:D_OUT], in0=result[:, BANK:D_OUT], in1=m_right[:], op=ALU.mult
+            )
             nc.sync.dma_start(out=out_rows[:, j, :], in_=result[:])
 
         adapter_tile(0)

@@ -23,8 +23,7 @@ OUT_TILES = D_OUT // P
 LOAD_TILES = 4
 PAIRS = TOKEN_TILES // 2
 AHEAD = 2
-LAG = 2
-HALVES = D_OUT // BANK
+SIDE_TILES = BANK // P
 
 FLOPS = 2 * TOKENS * D_OUT * (D_IN + RANK) + 2 * D_OUT * RANK * D_IN
 
@@ -38,7 +37,7 @@ def tile_loralinear_pa_t_kernel(tc, x, weight, a_w, b_w, magnitude, h_lora, out)
     with ExitStack() as stack:
         keep = stack.enter_context(tc.tile_pool(name="keep", bufs=1))
         work = stack.enter_context(tc.tile_pool(name="work", bufs=2))
-        psum = stack.enter_context(tc.psum_pool(name="psum", bufs=7))
+        psum = stack.enter_context(tc.psum_pool(name="psum", bufs=8))
         stack.enter_context(tc.manual_schedule())
 
         ident_bf16 = keep.tile([P, P], BF16)
@@ -183,79 +182,118 @@ def tile_loralinear_pa_t_kernel(tc, x, weight, a_w, b_w, magnitude, h_lora, out)
         m_col = keep.tile([P, OUT_TILES], F32)
         nc.vector.reciprocal(m_col[:], norm[:])
         nc.vector.tensor_tensor(out=m_col[:], in0=m_col[:], in1=mag_col[:], op=ALU.mult)
-        m_rep = keep.tile([P, D_OUT], F32)
-        nc.vector.tensor_copy(
-            out=m_rep[:].rearrange("p (a t) -> p a t", a=OUT_TILES),
-            in_=m_col[:].unsqueeze(2).to_broadcast([P, OUT_TILES, P]),
-        )
-        m_left = psum.tile([P, BANK], F32, tag="m", bufs=1)
-        m_right = keep.tile([P, BANK], F32)
+        m_all = keep.tile([P, D_OUT], F32)
 
-        def spread_m():
-            m_right_bank = psum.tile([P, BANK], F32, tag="ring")
-            for n, m_bank in enumerate((m_left, m_right_bank)):
-                for i in range(BANK // P):
-                    a = n * (BANK // P) + i
-                    nc.tensor.transpose(
-                        m_bank[:, i * P : (i + 1) * P], m_rep[:, a * P : (a + 1) * P], ident_f32[:]
-                    )
-            nc.scalar.copy(out=m_right[:], in_=m_right_bank[:])
+        def spread_m(half):
+            m_bank = psum.tile([P, BANK], F32, tag="ring", name="m_bank")
+            for i in range(SIDE_TILES):
+                a = half * SIDE_TILES + i
+                nc.tensor.transpose(
+                    m_bank[:, i * P : (i + 1) * P],
+                    m_col[:, a : a + 1].to_broadcast([P, P]),
+                    ident_f32[:],
+                )
+            nc.scalar.copy(out=m_all[:, half * BANK : (half + 1) * BANK], in_=m_bank[:])
 
+        LEFT = slice(0, BANK)
+        RIGHT = slice(BANK, D_OUT)
+        lora_sb = {}
+        baseT_sb = {}
+        base_left = {}
+        sum_right = {}
         results = {}
 
-        lora_sb = {}
+        def adapter_left(j):
+            lora = psum.tile([P, BANK], F32, tag="ring", name="lora")
+            nc.tensor.matmul(
+                lora[:], lhsT=hT[:, j * P : (j + 1) * P], rhs=bwT2[:, LEFT], start=True, stop=True
+            )
+            lora_sb[j] = work.tile([P, BANK], F32, tag="lsb", name="lora_sb", bufs=4)
+            nc.scalar.copy(out=lora_sb[j][:], in_=lora[:])
 
-        def adapter_tile(j):
+        def product_right(q):
+            tokens = slice(2 * q * P, (2 * q + 2) * P)
+            baseT_sb[q] = work.tile([P, SIDE_TILES, 2 * P], F32, tag="bT", name="baseT_sb", bufs=3)
+            for b in range(2):
+                bank = psum.tile([P, 2, 2 * P], F32, tag="ring", name="baseT")
+                for i in range(2):
+                    a = SIDE_TILES + 2 * b + i
+                    nc.tensor.matmul_mx(
+                        out=bank[:, i, :],
+                        lhsT=w_codes[:, a * P : (a + 1) * P].bitcast(FP8X4),
+                        lhsT_scale=w_scales[:, a * P : (a + 1) * P],
+                        rhs=x_codes[:, tokens].bitcast(FP8X4),
+                        rhs_scale=x_scales[:, tokens],
+                        start=True,
+                        stop=True,
+                    )
+                nc.scalar.copy(out=baseT_sb[q][:, 2 * b : 2 * b + 2, :], in_=bank[:])
+
+        def product_left(j):
             rows = slice(j * P, (j + 1) * P)
-            for n in range(HALVES):
-                cols = slice(n * BANK, (n + 1) * BANK)
-                lora = psum.tile([P, BANK], F32, tag="ring", name="lora")
-                nc.tensor.matmul(lora[:], lhsT=hT[:, rows], rhs=bwT2[:, cols], start=True, stop=True)
-                lora_sb[j, n] = work.tile([P, BANK], F32, tag="lsb", name="lora_sb", bufs=6)
-                nc.scalar.copy(out=lora_sb[j, n][:], in_=lora[:])
+            base_left[j] = psum.tile([P, BANK], F32, tag="ring", name="base")
+            nc.tensor.matmul_mx(
+                out=base_left[j][:],
+                lhsT=x_codes[:, rows].bitcast(FP8X4),
+                lhsT_scale=x_scales[:, rows],
+                rhs=w_codes[:, LEFT].bitcast(FP8X4),
+                rhs_scale=w_scales[:, LEFT],
+                start=True,
+                stop=True,
+            )
 
-        def sum_tile(j):
-            rows = slice(j * P, (j + 1) * P)
-            results[j] = work.tile([P, D_OUT], F32, tag="res", name="result", bufs=8)
-            for n in range(HALVES):
-                cols = slice(n * BANK, (n + 1) * BANK)
-                base = psum.tile([P, BANK], F32, tag="ring", name="base")
-                nc.tensor.matmul_mx(
-                    out=base[:],
-                    lhsT=x_codes[:, rows].bitcast(FP8X4),
-                    lhsT_scale=x_scales[:, rows],
-                    rhs=w_codes[:, cols].bitcast(FP8X4),
-                    rhs_scale=w_scales[:, cols],
-                    start=True,
-                    stop=True,
-                )
-                nc.vector.tensor_tensor(
-                    out=results[j][:, cols], in0=base[:], in1=lora_sb[j, n][:], op=ALU.add
+        def adapter_plus_product_right(j):
+            q, i = divmod(j, 2)
+            sum_right[j] = psum.tile([P, BANK], F32, tag="ring", name="total")
+            nc.tensor.matmul(
+                sum_right[j][:],
+                lhsT=hT[:, j * P : (j + 1) * P],
+                rhs=bwT2[:, RIGHT],
+                start=True,
+                stop=False,
+            )
+            for a in range(SIDE_TILES):
+                nc.tensor.matmul(
+                    sum_right[j][:, a * P : (a + 1) * P],
+                    lhsT=baseT_sb[q][:, a, i * P : (i + 1) * P],
+                    rhs=ident_f32[:],
+                    is_transpose=True,
+                    start=False,
+                    stop=a == SIDE_TILES - 1,
                 )
 
-        def scale_and_store(j):
-            result = results[j]
+        def finish_tile(j):
+            result = work.tile([P, D_OUT], F32, tag="res", name="result", bufs=8)
             nc.vector.tensor_tensor(
-                out=result[:, 0:BANK], in0=result[:, 0:BANK], in1=m_left[:], op=ALU.mult
+                out=result[:, LEFT], in0=base_left[j][:], in1=lora_sb[j][:], op=ALU.add
             )
             nc.gpsimd.tensor_tensor(
-                out=result[:, BANK:D_OUT], in0=result[:, BANK:D_OUT], in1=m_right[:], op=ALU.mult
+                out=result[:, LEFT], in0=result[:, LEFT], in1=m_all[:, LEFT], op=ALU.mult
+            )
+            nc.vector.tensor_tensor(
+                out=result[:, RIGHT], in0=sum_right[j][:], in1=m_all[:, RIGHT], op=ALU.mult
             )
             nc.sync.dma_start(out=out_rows[:, j, :], in_=result[:])
 
-        adapter_tile(0)
-        for j in range(TOKEN_TILES + LAG):
-            if j < TOKEN_TILES:
-                q_next = j // 2 + AHEAD
-                prepares = j % 2 == 0 and q_next < PAIRS
-                if prepares:
-                    prepare_token_pair(q_next, nc.scalar.copy)
-                if j + 1 < TOKEN_TILES:
-                    adapter_tile(j + 1)
-                sum_tile(j)
-                if prepares:
-                    quantise_token_pair(q_next)
-            if j == LAG - 1:
-                spread_m()
-            if j >= LAG:
-                scale_and_store(j - LAG)
+        product_right(0)
+        for j in range(2):
+            adapter_left(j)
+        for half in range(2):
+            spread_m(half)
+        for q in range(PAIRS):
+            pair_tiles = (2 * q, 2 * q + 1)
+            if q + AHEAD < PAIRS:
+                prepare_token_pair(q + AHEAD, nc.scalar.copy)
+            if q + 1 < PAIRS:
+                product_right(q + 1)
+            for j in pair_tiles:
+                product_left(j)
+            if q + 1 < PAIRS:
+                for j in pair_tiles:
+                    adapter_left(j + 2)
+            for j in pair_tiles:
+                adapter_plus_product_right(j)
+            finish_tile(2 * q)
+            if q + AHEAD < PAIRS:
+                quantise_token_pair(q + AHEAD)
+            finish_tile(2 * q + 1)

@@ -242,8 +242,7 @@ def tile_loralinear_pa_t_kernel(tc, x, weight, a_w, b_w, magnitude, h_lora, out)
                 stop=True,
             )
 
-        def adapter_plus_product_right(j):
-            q, i = divmod(j, 2)
+        def adapter_right(j):
             sum_right[j] = psum.tile([P, BANK], F32, tag="ring", name="total")
             nc.tensor.matmul(
                 sum_right[j][:],
@@ -252,6 +251,9 @@ def tile_loralinear_pa_t_kernel(tc, x, weight, a_w, b_w, magnitude, h_lora, out)
                 start=True,
                 stop=False,
             )
+
+        def add_product_right(j):
+            q, i = divmod(j, 2)
             for a in range(SIDE_TILES):
                 nc.tensor.matmul(
                     sum_right[j][:, a * P : (a + 1) * P],
@@ -292,7 +294,9 @@ def tile_loralinear_pa_t_kernel(tc, x, weight, a_w, b_w, magnitude, h_lora, out)
                 for j in pair_tiles:
                     adapter_left(j + 2)
             for j in pair_tiles:
-                adapter_plus_product_right(j)
+                adapter_right(j)
+            for j in pair_tiles:
+                add_product_right(j)
             finish_tile(2 * q)
             if q + AHEAD < PAIRS:
                 quantise_token_pair(q + AHEAD)

@@ -22,7 +22,7 @@ TOKEN_TILES = TOKENS // P
 OUT_TILES = D_OUT // P
 LOAD_TILES = 4
 PAIRS = TOKEN_TILES // 2
-AHEAD = 2
+AHEAD = 3
 SIDE_TILES = BANK // P
 
 FLOPS = 2 * TOKENS * D_OUT * (D_IN + RANK) + 2 * D_OUT * RANK * D_IN
@@ -37,7 +37,7 @@ def tile_loralinear_pa_t_kernel(tc, x, weight, a_w, b_w, magnitude, h_lora, out)
     with ExitStack() as stack:
         keep = stack.enter_context(tc.tile_pool(name="keep", bufs=1))
         work = stack.enter_context(tc.tile_pool(name="work", bufs=2))
-        psum = stack.enter_context(tc.psum_pool(name="psum", bufs=8))
+        psum = stack.enter_context(tc.psum_pool(name="psum", bufs=7))
         stack.enter_context(tc.manual_schedule())
 
         ident_bf16 = keep.tile([P, P], BF16)
@@ -112,8 +112,8 @@ def tile_loralinear_pa_t_kernel(tc, x, weight, a_w, b_w, magnitude, h_lora, out)
         hT = keep.tile([P, TOKENS], BF16)
         x_grouped = {}
 
-        def prepare_token_pair(q, copy):
-            x_grouped[q] = work.tile([P, 2 * P * 4], BF16, align_bytes=64, tag="xg", name="x_grouped")
+        def transpose_token_pair(q, copy):
+            x_grouped[q] = work.tile([P, 2 * P * 4], BF16, align_bytes=64, tag="xg", name="x_grouped", bufs=3)
             regroup_two_row_tiles(x_sb[:].bitcast(F32), 2 * q, x_grouped[q][:].bitcast(F32), copy)
             h_bank = psum.tile([P, 2 * P], BF16, tag="ring", name="h_bank")
             for i in range(2):
@@ -165,8 +165,8 @@ def tile_loralinear_pa_t_kernel(tc, x, weight, a_w, b_w, magnitude, h_lora, out)
                 nc.scalar.activation(
                     out=squares[:], in_=w_eff[:], func=ACT.Square, accum_out=norm_sq[:, a : a + 1]
                 )
-            if pair >= OUT_TILES // 2 - AHEAD:
-                prepare_token_pair(pair - (OUT_TILES // 2 - AHEAD), nc.vector.tensor_copy)
+            if pair >= OUT_TILES // 2 - 2:
+                transpose_token_pair(pair - (OUT_TILES // 2 - 2), nc.vector.tensor_copy)
             if pair % 2 == 1:
                 half = pair // 2
                 nc.vector.quantize_mx(
@@ -174,7 +174,7 @@ def tile_loralinear_pa_t_kernel(tc, x, weight, a_w, b_w, magnitude, h_lora, out)
                     scales=w_scales[:, half * BANK : (half + 1) * BANK],
                     in_=w_grouped[:, half * BANK * 4 : (half + 1) * BANK * 4],
                 )
-        for q in range(AHEAD):
+        for q in range(2):
             quantise_token_pair(q)
 
         norm = keep.tile([P, OUT_TILES], F32)
@@ -183,121 +183,137 @@ def tile_loralinear_pa_t_kernel(tc, x, weight, a_w, b_w, magnitude, h_lora, out)
         nc.vector.reciprocal(m_col[:], norm[:])
         nc.vector.tensor_tensor(out=m_col[:], in0=m_col[:], in1=mag_col[:], op=ALU.mult)
         m_all = keep.tile([P, D_OUT], F32)
+        m_right = psum.tile([P, BANK], F32, tag="m", bufs=1)
 
-        def spread_m(half):
-            m_bank = psum.tile([P, BANK], F32, tag="ring", name="m_bank")
-            for i in range(SIDE_TILES):
-                a = half * SIDE_TILES + i
-                nc.tensor.transpose(
-                    m_bank[:, i * P : (i + 1) * P],
-                    m_col[:, a : a + 1].to_broadcast([P, P]),
-                    ident_f32[:],
-                )
-            nc.scalar.copy(out=m_all[:, half * BANK : (half + 1) * BANK], in_=m_bank[:])
+        def spread_m():
+            m_left = psum.tile([P, BANK], F32, tag="ring", name="m_left")
+            for half, m_bank in ((1, m_right), (0, m_left)):
+                for i in range(SIDE_TILES):
+                    a = half * SIDE_TILES + i
+                    nc.tensor.transpose(
+                        m_bank[:, i * P : (i + 1) * P],
+                        m_col[:, a : a + 1].to_broadcast([P, P]),
+                        ident_f32[:],
+                    )
+                nc.scalar.copy(out=m_all[:, half * BANK : (half + 1) * BANK], in_=m_bank[:])
 
         LEFT = slice(0, BANK)
         RIGHT = slice(BANK, D_OUT)
         lora_sb = {}
         baseT_sb = {}
-        base_left = {}
-        sum_right = {}
+        base = {}
+        total = {}
         results = {}
 
-        def adapter_left(j):
+        def adapter(j, side):
             lora = psum.tile([P, BANK], F32, tag="ring", name="lora")
             nc.tensor.matmul(
-                lora[:], lhsT=hT[:, j * P : (j + 1) * P], rhs=bwT2[:, LEFT], start=True, stop=True
+                lora[:], lhsT=hT[:, j * P : (j + 1) * P], rhs=bwT2[:, side], start=True, stop=True
             )
-            lora_sb[j] = work.tile([P, BANK], F32, tag="lsb", name="lora_sb", bufs=4)
-            nc.scalar.copy(out=lora_sb[j][:], in_=lora[:])
+            lora_sb[j, side.start] = work.tile([P, BANK], F32, tag="lsb", name="lora_sb", bufs=6)
+            nc.scalar.copy(out=lora_sb[j, side.start][:], in_=lora[:])
 
-        def product_right(q):
-            tokens = slice(2 * q * P, (2 * q + 2) * P)
-            baseT_sb[q] = work.tile([P, SIDE_TILES, 2 * P], F32, tag="bT", name="baseT_sb", bufs=3)
-            for b in range(2):
-                bank = psum.tile([P, 2, 2 * P], F32, tag="ring", name="baseT")
-                for i in range(2):
-                    a = SIDE_TILES + 2 * b + i
-                    nc.tensor.matmul_mx(
-                        out=bank[:, i, :],
-                        lhsT=w_codes[:, a * P : (a + 1) * P].bitcast(FP8X4),
-                        lhsT_scale=w_scales[:, a * P : (a + 1) * P],
-                        rhs=x_codes[:, tokens].bitcast(FP8X4),
-                        rhs_scale=x_scales[:, tokens],
-                        start=True,
-                        stop=True,
-                    )
-                nc.scalar.copy(out=baseT_sb[q][:, 2 * b : 2 * b + 2, :], in_=bank[:])
+        def product_turned(j):
+            tokens = slice(j * P, (j + 1) * P)
+            bank = psum.tile([P, SIDE_TILES * P], F32, tag="ring", name="baseT")
+            for i in range(SIDE_TILES):
+                a = SIDE_TILES + i
+                nc.tensor.matmul_mx(
+                    out=bank[:, i * P : (i + 1) * P],
+                    lhsT=w_codes[:, a * P : (a + 1) * P].bitcast(FP8X4),
+                    lhsT_scale=w_scales[:, a * P : (a + 1) * P],
+                    rhs=x_codes[:, tokens].bitcast(FP8X4),
+                    rhs_scale=x_scales[:, tokens],
+                    start=True,
+                    stop=True,
+                )
+            baseT_sb[j] = work.tile([P, SIDE_TILES * P], F32, tag="bT", name="baseT_sb", bufs=3)
+            nc.scalar.copy(out=baseT_sb[j][:], in_=bank[:])
 
-        def product_left(j):
+        def product(j, side):
             rows = slice(j * P, (j + 1) * P)
-            base_left[j] = psum.tile([P, BANK], F32, tag="ring", name="base")
+            base[j, side.start] = psum.tile([P, BANK], F32, tag="ring", name="base")
             nc.tensor.matmul_mx(
-                out=base_left[j][:],
+                out=base[j, side.start][:],
                 lhsT=x_codes[:, rows].bitcast(FP8X4),
                 lhsT_scale=x_scales[:, rows],
-                rhs=w_codes[:, LEFT].bitcast(FP8X4),
-                rhs_scale=w_scales[:, LEFT],
+                rhs=w_codes[:, side].bitcast(FP8X4),
+                rhs_scale=w_scales[:, side],
                 start=True,
                 stop=True,
             )
 
-        def adapter_right(j):
-            sum_right[j] = psum.tile([P, BANK], F32, tag="ring", name="total")
+        def open_total(j):
+            total[j] = psum.tile([P, BANK], F32, tag="ring", name="total")
             nc.tensor.matmul(
-                sum_right[j][:],
+                total[j][:],
                 lhsT=hT[:, j * P : (j + 1) * P],
                 rhs=bwT2[:, RIGHT],
                 start=True,
                 stop=False,
             )
 
-        def add_product_right(j):
-            q, i = divmod(j, 2)
+        def add_turned_product(j):
             for a in range(SIDE_TILES):
                 nc.tensor.matmul(
-                    sum_right[j][:, a * P : (a + 1) * P],
-                    lhsT=baseT_sb[q][:, a, i * P : (i + 1) * P],
+                    total[j][:, a * P : (a + 1) * P],
+                    lhsT=baseT_sb[j][:, a * P : (a + 1) * P],
                     rhs=ident_f32[:],
                     is_transpose=True,
                     start=False,
                     stop=a == SIDE_TILES - 1,
                 )
 
-        def finish_tile(j):
-            result = work.tile([P, D_OUT], F32, tag="res", name="result", bufs=8)
+        def add(j, side):
             nc.vector.tensor_tensor(
-                out=result[:, LEFT], in0=base_left[j][:], in1=lora_sb[j][:], op=ALU.add
+                out=results[j][:, side],
+                in0=base[j, side.start][:],
+                in1=lora_sb[j, side.start][:],
+                op=ALU.add,
             )
-            nc.gpsimd.tensor_tensor(
-                out=result[:, LEFT], in0=result[:, LEFT], in1=m_all[:, LEFT], op=ALU.mult
-            )
-            nc.vector.tensor_tensor(
-                out=result[:, RIGHT], in0=sum_right[j][:], in1=m_all[:, RIGHT], op=ALU.mult
-            )
-            nc.sync.dma_start(out=out_rows[:, j, :], in_=result[:])
 
-        product_right(0)
-        for j in range(2):
-            adapter_left(j)
-        for half in range(2):
-            spread_m(half)
+        def scale_left(j):
+            nc.gpsimd.tensor_tensor(
+                out=results[j][:, LEFT], in0=results[j][:, LEFT], in1=m_all[:, LEFT], op=ALU.mult
+            )
+
+        def store(j):
+            nc.sync.dma_start(out=out_rows[:, j, :], in_=results[j][:])
+
+        def adapters_of_pair(q):
+            for j, side in ((2 * q, LEFT), (2 * q + 1, LEFT), (2 * q + 1, RIGHT)):
+                adapter(j, side)
+
+        product_turned(0)
+        adapters_of_pair(0)
+        spread_m()
+        transpose_token_pair(2, nc.scalar.copy)
         for q in range(PAIRS):
-            pair_tiles = (2 * q, 2 * q + 1)
-            if q + AHEAD < PAIRS:
-                prepare_token_pair(q + AHEAD, nc.scalar.copy)
+            even, odd = 2 * q, 2 * q + 1
+            for j in (even, odd):
+                results[j] = work.tile([P, D_OUT], F32, tag="res", name="result", bufs=8)
             if q + 1 < PAIRS:
-                product_right(q + 1)
-            for j in pair_tiles:
-                product_left(j)
+                product_turned(even + 2)
+            for j, side in ((even, LEFT), (odd, RIGHT), (odd, LEFT)):
+                product(j, side)
+            open_total(even)
             if q + 1 < PAIRS:
-                for j in pair_tiles:
-                    adapter_left(j + 2)
-            for j in pair_tiles:
-                adapter_right(j)
-            for j in pair_tiles:
-                add_product_right(j)
-            finish_tile(2 * q)
+                adapters_of_pair(q + 1)
+            add_turned_product(even)
             if q + AHEAD < PAIRS:
-                quantise_token_pair(q + AHEAD)
-            finish_tile(2 * q + 1)
+                transpose_token_pair(q + AHEAD, nc.scalar.copy)
+            add(even, LEFT)
+            scale_left(even)
+            if q + 2 < PAIRS:
+                quantise_token_pair(q + 2)
+            add(odd, RIGHT)
+            add(odd, LEFT)
+            scale_left(odd)
+            nc.vector.tensor_tensor(
+                out=results[odd][:, RIGHT], in0=results[odd][:, RIGHT], in1=m_right[:], op=ALU.mult
+            )
+            nc.vector.tensor_tensor(
+                out=results[even][:, RIGHT], in0=total[even][:], in1=m_all[:, RIGHT], op=ALU.mult
+            )
+            store(even)
+            store(odd)

@@ -40,19 +40,19 @@ def tile_loralinear_pa_t_kernel(tc, x, weight, a_w, b_w, magnitude, h_lora, out)
         psum = stack.enter_context(tc.psum_pool(name="psum", bufs=7))
         stack.enter_context(tc.manual_schedule())
 
-        ident_bf16 = keep.tile([P, P], BF16)
+        ident_bf16 = keep.tile([P, P], BF16, align_bytes=256)
         make_identity(nc, ident_bf16[:])
-        ident_f32 = keep.tile([P, P], F32)
+        ident_f32 = keep.tile([P, P], F32, align_bytes=256)
         make_identity(nc, ident_f32[:])
         one = keep.tile([P, 1], F32)
         nc.vector.memset(one[:], 1.0)
         nc.scalar.sqrt(one[:], one[:])
 
-        w_sb = keep.tile([P, OUT_TILES * D_IN], BF16)
-        x_sb = keep.tile([P, TOKEN_TILES * D_IN], BF16)
-        h_sb = keep.tile([P, TOKEN_TILES * RANK], BF16)
-        bw_sb = keep.tile([P, OUT_TILES * RANK], BF16)
-        aw_sb = keep.tile([P, D_IN], BF16)
+        w_sb = keep.tile([P, OUT_TILES * D_IN], BF16, align_bytes=256)
+        x_sb = keep.tile([P, TOKEN_TILES * D_IN], BF16, align_bytes=256)
+        h_sb = keep.tile([P, TOKEN_TILES * RANK], BF16, align_bytes=256)
+        bw_sb = keep.tile([P, OUT_TILES * RANK], BF16, align_bytes=256)
+        aw_sb = keep.tile([P, D_IN], BF16, align_bytes=256)
         mag_rows = keep.tile([P, P], BF16)
         nc.vector.memset(mag_rows[:], 0.0)
 
@@ -71,8 +71,8 @@ def tile_loralinear_pa_t_kernel(tc, x, weight, a_w, b_w, magnitude, h_lora, out)
             cols = slice(c * LOAD_TILES * D_IN, (c + 1) * LOAD_TILES * D_IN)
             nc.sync.dma_start(out=x_sb[:, cols], in_=x_rows[:, cols])
 
-        def load_h_half(half):
-            cols = slice(half * TOKEN_TILES // 2 * RANK, (half + 1) * TOKEN_TILES // 2 * RANK)
+        def load_h(c):
+            cols = slice(c * 2 * LOAD_TILES * RANK, (c + 1) * 2 * LOAD_TILES * RANK)
             nc.sync.dma_start(out=h_sb[:, cols], in_=h_rows[:, cols])
 
         nc.sync.dma_start(
@@ -85,13 +85,10 @@ def tile_loralinear_pa_t_kernel(tc, x, weight, a_w, b_w, magnitude, h_lora, out)
         load_weight_half(0)
         nc.sync.dma_start(out=aw_sb[:], in_=a_w)
         load_weight_half(1)
-        load_x(0)
-        load_h_half(0)
-        load_x(1)
-        load_x(2)
-        load_h_half(1)
-        for c in range(3, TOKEN_TILES // LOAD_TILES):
+        for c in range(TOKEN_TILES // LOAD_TILES):
             load_x(c)
+            if c % 2 == 0:
+                load_h(c // 2)
 
         def regroup_two_row_tiles(words, first_tile, grouped_words, copy):
             bank = psum.tile([P, 2, 2, P], F32, tag="ring", name="bank")
@@ -104,12 +101,12 @@ def tile_loralinear_pa_t_kernel(tc, x, weight, a_w, b_w, magnitude, h_lora, out)
                 in_=bank[:].rearrange("p i u r -> p i r u"),
             )
 
-        w_codes = keep.tile([P, D_OUT], U32, align_bytes=64)
-        w_scales = keep.tile([P, D_OUT], U8, align_bytes=64)
-        w_grouped = keep.tile([P, D_OUT * 4], BF16, align_bytes=64)
-        x_codes = keep.tile([P, TOKENS], U32, align_bytes=64)
-        x_scales = keep.tile([P, TOKENS], U8, align_bytes=64)
-        hT = keep.tile([P, TOKENS], BF16)
+        w_codes = keep.tile([P, D_OUT], U32, align_bytes=256)
+        w_scales = keep.tile([P, D_OUT], U8, align_bytes=256)
+        w_grouped = keep.tile([P, D_OUT * 4], BF16, align_bytes=256)
+        x_codes = keep.tile([P, TOKENS], U32, align_bytes=256)
+        x_scales = keep.tile([P, TOKENS], U8, align_bytes=256)
+        hT = keep.tile([P, TOKENS], BF16, align_bytes=256)
         x_grouped = {}
 
         def transpose_token_pair(q, copy):
@@ -129,53 +126,77 @@ def tile_loralinear_pa_t_kernel(tc, x, weight, a_w, b_w, magnitude, h_lora, out)
                 out=x_codes[:, cols].bitcast(FP8X4), scales=x_scales[:, cols], in_=x_grouped[q][:]
             )
 
-        bw_bank = psum.tile([P, D_OUT], BF16, tag="ring", name="bw_bank")
-        for a in range(OUT_TILES):
-            nc.tensor.transpose(
-                bw_bank[:, a * P : (a + 1) * P], bw_sb[:, a * RANK : (a + 1) * RANK], ident_bf16[:]
-            )
-        bwT2 = keep.tile([P, D_OUT], BF16)
-        nc.scalar.mul(out=bwT2[:], in_=bw_bank[:], mul=2.0)
-        mag_bank = psum.tile([P, P], BF16, tag="ring", name="mag_bank")
-        nc.tensor.transpose(mag_bank[:], mag_rows[:], ident_bf16[:])
-        mag_col = keep.tile([P, OUT_TILES], F32)
-        nc.vector.tensor_copy(out=mag_col[:], in_=mag_bank[:, 0:OUT_TILES])
+        bwT2 = keep.tile([P, D_OUT], BF16, align_bytes=256)
+        bw_banks = []
+        for half in range(2):
+            bw_bank = psum.tile([P, BANK], BF16, tag="ring", name="bw_bank")
+            for i in range(SIDE_TILES):
+                a = half * SIDE_TILES + i
+                nc.tensor.transpose(
+                    bw_bank[:, i * P : (i + 1) * P], bw_sb[:, a * RANK : (a + 1) * RANK], ident_bf16[:]
+                )
+            bw_banks.append(bw_bank)
+        nc.scalar.mul(out=bwT2[:, 0:BANK], in_=bw_banks[0][:], mul=2.0)
+        nc.vector.tensor_scalar(
+            out=bwT2[:, BANK:D_OUT], in0=bw_banks[1][:], scalar1=2.0, scalar2=None, op0=ALU.mult
+        )
 
         norm_sq = keep.tile([P, OUT_TILES], F32)
-        for pair in range(OUT_TILES // 2):
+
+        def regroup_weight_pair(pair):
             regroup_two_row_tiles(
                 w_sb[:].bitcast(F32),
                 2 * pair,
                 w_grouped[:].bitcast(F32)[:, pair * BANK : (pair + 1) * BANK],
                 nc.vector.tensor_copy,
             )
-            for a in (2 * pair, 2 * pair + 1):
-                w_eff = psum.tile([P, D_IN], F32, tag="ring", name="w_eff")
-                nc.tensor.matmul(
-                    w_eff[:], lhsT=bwT2[:, a * P : (a + 1) * P], rhs=aw_sb[:], start=True, stop=False
-                )
-                nc.tensor.matmul(
-                    w_eff[:],
-                    lhsT=ident_bf16[:],
-                    rhs=w_sb[:, a * D_IN : (a + 1) * D_IN],
-                    start=False,
-                    stop=True,
-                )
-                squares = work.tile([P, D_IN], F32, tag="sq", name="squares")
-                nc.scalar.activation(
-                    out=squares[:], in_=w_eff[:], func=ACT.Square, accum_out=norm_sq[:, a : a + 1]
-                )
-            if pair >= OUT_TILES // 2 - 2:
-                transpose_token_pair(pair - (OUT_TILES // 2 - 2), nc.vector.tensor_copy)
-            if pair % 2 == 1:
-                half = pair // 2
-                nc.vector.quantize_mx(
-                    out=w_codes[:, half * BANK : (half + 1) * BANK].bitcast(FP8X4),
-                    scales=w_scales[:, half * BANK : (half + 1) * BANK],
-                    in_=w_grouped[:, half * BANK * 4 : (half + 1) * BANK * 4],
-                )
-        for q in range(2):
-            quantise_token_pair(q)
+
+        def quantise_weight_half(half):
+            nc.vector.quantize_mx(
+                out=w_codes[:, half * BANK : (half + 1) * BANK].bitcast(FP8X4),
+                scales=w_scales[:, half * BANK : (half + 1) * BANK],
+                in_=w_grouped[:, half * BANK * 4 : (half + 1) * BANK * 4],
+            )
+
+        def square_norms(a):
+            w_eff = psum.tile([P, D_IN], F32, tag="ring", name="w_eff")
+            nc.tensor.matmul(
+                w_eff[:], lhsT=bwT2[:, a * P : (a + 1) * P], rhs=aw_sb[:], start=True, stop=False
+            )
+            nc.tensor.matmul(
+                w_eff[:],
+                lhsT=ident_bf16[:],
+                rhs=w_sb[:, a * D_IN : (a + 1) * D_IN],
+                start=False,
+                stop=True,
+            )
+            squares = work.tile([P, D_IN], F32, tag="sq", name="squares")
+            nc.scalar.activation(
+                out=squares[:], in_=w_eff[:], func=ACT.Square, accum_out=norm_sq[:, a : a + 1]
+            )
+
+        regroup_weight_pair(0)
+        square_norms(0)
+        square_norms(1)
+        regroup_weight_pair(1)
+        square_norms(2)
+        square_norms(3)
+        regroup_weight_pair(2)
+        quantise_weight_half(0)
+        square_norms(4)
+        square_norms(5)
+        regroup_weight_pair(3)
+        square_norms(6)
+        transpose_token_pair(0, nc.vector.tensor_copy)
+        square_norms(7)
+        quantise_token_pair(0)
+        quantise_weight_half(1)
+        transpose_token_pair(1, nc.vector.tensor_copy)
+        quantise_token_pair(1)
+        mag_bank = psum.tile([P, P], BF16, tag="ring", name="mag_bank")
+        nc.tensor.transpose(mag_bank[:], mag_rows[:], ident_bf16[:])
+        mag_col = keep.tile([P, OUT_TILES], F32)
+        nc.vector.tensor_copy(out=mag_col[:], in_=mag_bank[:, 0:OUT_TILES])
 
         norm = keep.tile([P, OUT_TILES], F32)
         nc.scalar.sqrt(norm[:], norm_sq[:])
@@ -185,17 +206,15 @@ def tile_loralinear_pa_t_kernel(tc, x, weight, a_w, b_w, magnitude, h_lora, out)
         m_all = keep.tile([P, D_OUT], F32)
         m_right = psum.tile([P, BANK], F32, tag="m", bufs=1)
 
-        def spread_m():
-            m_left = psum.tile([P, BANK], F32, tag="ring", name="m_left")
-            for half, m_bank in ((1, m_right), (0, m_left)):
-                for i in range(SIDE_TILES):
-                    a = half * SIDE_TILES + i
-                    nc.tensor.transpose(
-                        m_bank[:, i * P : (i + 1) * P],
-                        m_col[:, a : a + 1].to_broadcast([P, P]),
-                        ident_f32[:],
-                    )
-                nc.scalar.copy(out=m_all[:, half * BANK : (half + 1) * BANK], in_=m_bank[:])
+        def spread_m(half, m_bank):
+            for i in range(SIDE_TILES):
+                a = half * SIDE_TILES + i
+                nc.tensor.transpose(
+                    m_bank[:, i * P : (i + 1) * P],
+                    m_col[:, a : a + 1].to_broadcast([P, P]),
+                    ident_f32[:],
+                )
+            nc.scalar.copy(out=m_all[:, half * BANK : (half + 1) * BANK], in_=m_bank[:])
 
         LEFT = slice(0, BANK)
         RIGHT = slice(BANK, D_OUT)
@@ -227,7 +246,7 @@ def tile_loralinear_pa_t_kernel(tc, x, weight, a_w, b_w, magnitude, h_lora, out)
                     start=True,
                     stop=True,
                 )
-            baseT_sb[j] = work.tile([P, SIDE_TILES * P], F32, tag="bT", name="baseT_sb", bufs=3)
+            baseT_sb[j] = work.tile([P, SIDE_TILES * P], F32, tag="bT", name="baseT_sb", bufs=3, align_bytes=256)
             nc.scalar.copy(out=baseT_sb[j][:], in_=bank[:])
 
         def product(j, side):
@@ -284,18 +303,25 @@ def tile_loralinear_pa_t_kernel(tc, x, weight, a_w, b_w, magnitude, h_lora, out)
             for j, side in ((2 * q, LEFT), (2 * q + 1, LEFT), (2 * q + 1, RIGHT)):
                 adapter(j, side)
 
-        product_turned(0)
+        def products_of_pair(q):
+            for j, side in ((2 * q, LEFT), (2 * q + 1, LEFT), (2 * q + 1, RIGHT)):
+                product(j, side)
+
         adapters_of_pair(0)
-        spread_m()
-        transpose_token_pair(2, nc.scalar.copy)
+        products_of_pair(0)
+        transpose_token_pair(2, nc.vector.tensor_copy)
+        m_left = psum.tile([P, BANK], F32, tag="ring", name="m_left")
+        spread_m(0, m_left)
+        product_turned(0)
+        spread_m(1, m_right)
         for q in range(PAIRS):
             even, odd = 2 * q, 2 * q + 1
             for j in (even, odd):
                 results[j] = work.tile([P, D_OUT], F32, tag="res", name="result", bufs=8)
             if q + 1 < PAIRS:
                 product_turned(even + 2)
-            for j, side in ((even, LEFT), (odd, RIGHT), (odd, LEFT)):
-                product(j, side)
+            if q > 0:
+                products_of_pair(q)
             open_total(even)
             if q + 1 < PAIRS:
                 adapters_of_pair(q + 1)
@@ -304,11 +330,11 @@ def tile_loralinear_pa_t_kernel(tc, x, weight, a_w, b_w, magnitude, h_lora, out)
                 transpose_token_pair(q + AHEAD, nc.scalar.copy)
             add(even, LEFT)
             scale_left(even)
-            if q + 2 < PAIRS:
-                quantise_token_pair(q + 2)
-            add(odd, RIGHT)
             add(odd, LEFT)
             scale_left(odd)
+            add(odd, RIGHT)
+            if q + 2 < PAIRS:
+                quantise_token_pair(q + 2)
             nc.vector.tensor_tensor(
                 out=results[odd][:, RIGHT], in0=results[odd][:, RIGHT], in1=m_right[:], op=ALU.mult
             )

@@ -330,11 +330,11 @@ def tile_loralinear_pa_t_kernel(tc, x, weight, a_w, b_w, magnitude, h_lora, out)
                 transpose_token_pair(q + AHEAD, nc.scalar.copy)
             add(even, LEFT)
             scale_left(even)
+            if q + 2 < PAIRS:
+                quantise_token_pair(q + 2)
             add(odd, LEFT)
             scale_left(odd)
             add(odd, RIGHT)
-            if q + 2 < PAIRS:
-                quantise_token_pair(q + 2)
             nc.vector.tensor_tensor(
                 out=results[odd][:, RIGHT], in0=results[odd][:, RIGHT], in1=m_right[:], op=ALU.mult
             )

@@ -23,6 +23,7 @@ OUT_TILES = D_OUT // P
 LOAD_TILES = 4
 PAIRS = TOKEN_TILES // 2
 AHEAD = 3
+WARM_UP = 4
 SIDE_TILES = BANK // P
 
 FLOPS = 2 * TOKENS * D_OUT * (D_IN + RANK) + 2 * D_OUT * RANK * D_IN
@@ -47,6 +48,12 @@ def tile_loralinear_pa_t_kernel(tc, x, weight, a_w, b_w, magnitude, h_lora, out)
         one = keep.tile([P, 1], F32)
         nc.vector.memset(one[:], 1.0)
         nc.scalar.sqrt(one[:], one[:])
+
+        zeros = keep.tile([P, BANK], BF16)
+        nc.vector.memset(zeros[:], 0.0)
+        warm = psum.tile([P, BANK], F32, tag="ring", name="warm")
+        for i in range(WARM_UP):
+            nc.tensor.matmul(warm[:], lhsT=zeros[:, 0:P], rhs=zeros[:], start=True, stop=True)
 
         w_sb = keep.tile([P, OUT_TILES * D_IN], BF16, align_bytes=256)
         x_sb = keep.tile([P, TOKEN_TILES * D_IN], BF16, align_bytes=256)
@@ -246,7 +253,7 @@ def tile_loralinear_pa_t_kernel(tc, x, weight, a_w, b_w, magnitude, h_lora, out)
                     start=True,
                     stop=True,
                 )
-            baseT_sb[j] = work.tile([P, SIDE_TILES * P], F32, tag="bT", name="baseT_sb", bufs=3, align_bytes=256)
+            baseT_sb[j] = work.tile([P, SIDE_TILES * P], F32, tag="bT", name="baseT_sb", bufs=4, align_bytes=256)
             nc.scalar.copy(out=baseT_sb[j][:], in_=bank[:])
 
         def product(j, side):
@@ -284,27 +291,36 @@ def tile_loralinear_pa_t_kernel(tc, x, weight, a_w, b_w, magnitude, h_lora, out)
                 )
 
         def add(j, side):
+            q, i = divmod(j, 2)
             nc.vector.tensor_tensor(
-                out=results[j][:, side],
+                out=results[q][:, i, side],
                 in0=base[j, side.start][:],
                 in1=lora_sb[j, side.start][:],
                 op=ALU.add,
             )
 
-        def scale_left(j):
+        def scale_left(q, first, end):
+            halves = results[q][:, first:end, LEFT]
             nc.gpsimd.tensor_tensor(
-                out=results[j][:, LEFT], in0=results[j][:, LEFT], in1=m_all[:, LEFT], op=ALU.mult
+                out=halves,
+                in0=halves,
+                in1=m_all[:, LEFT].unsqueeze(1).to_broadcast([P, end - first, BANK]),
+                op=ALU.mult,
             )
 
-        def store(j):
-            nc.sync.dma_start(out=out_rows[:, j, :], in_=results[j][:])
+        def turned_tiles(q):
+            return (2 * q, 2 * q + 1) if q >= PAIRS - 2 else (2 * q,)
+
+        def halves_for_vector(q):
+            rights = [(j, RIGHT) for j in (2 * q, 2 * q + 1) if j not in turned_tiles(q)]
+            return rights + [(2 * q, LEFT), (2 * q + 1, LEFT)]
 
         def adapters_of_pair(q):
-            for j, side in ((2 * q, LEFT), (2 * q + 1, LEFT), (2 * q + 1, RIGHT)):
+            for j, side in halves_for_vector(q):
                 adapter(j, side)
 
         def products_of_pair(q):
-            for j, side in ((2 * q, LEFT), (2 * q + 1, LEFT), (2 * q + 1, RIGHT)):
+            for j, side in halves_for_vector(q):
                 product(j, side)
 
         adapters_of_pair(0)
@@ -312,34 +328,45 @@ def tile_loralinear_pa_t_kernel(tc, x, weight, a_w, b_w, magnitude, h_lora, out)
         transpose_token_pair(2, nc.vector.tensor_copy)
         m_left = psum.tile([P, BANK], F32, tag="ring", name="m_left")
         spread_m(0, m_left)
-        product_turned(0)
+        for j in turned_tiles(0):
+            product_turned(j)
         spread_m(1, m_right)
         for q in range(PAIRS):
             even, odd = 2 * q, 2 * q + 1
-            for j in (even, odd):
-                results[j] = work.tile([P, D_OUT], F32, tag="res", name="result", bufs=8)
+            results[q] = work.tile([P, 2, D_OUT], F32, tag="res", name="result", bufs=4)
             if q + 1 < PAIRS:
-                product_turned(even + 2)
+                for j in turned_tiles(q + 1):
+                    product_turned(j)
             if q > 0:
                 products_of_pair(q)
-            open_total(even)
+            for j in turned_tiles(q):
+                open_total(j)
             if q + 1 < PAIRS:
                 adapters_of_pair(q + 1)
-            add_turned_product(even)
+            for j in turned_tiles(q):
+                add_turned_product(j)
             if q + AHEAD < PAIRS:
                 transpose_token_pair(q + AHEAD, nc.scalar.copy)
-            add(even, LEFT)
-            scale_left(even)
+            last = q == PAIRS - 1
+            for j, side in halves_for_vector(q):
+                add(j, side)
+                if last:
+                    scale_left(q, j % 2, j % 2 + 1)
+            if not last:
+                scale_left(q, 0, 2)
             if q + 2 < PAIRS:
                 quantise_token_pair(q + 2)
-            add(odd, LEFT)
-            scale_left(odd)
-            add(odd, RIGHT)
-            nc.vector.tensor_tensor(
-                out=results[odd][:, RIGHT], in0=results[odd][:, RIGHT], in1=m_right[:], op=ALU.mult
-            )
-            nc.vector.tensor_tensor(
-                out=results[even][:, RIGHT], in0=total[even][:], in1=m_all[:, RIGHT], op=ALU.mult
-            )
-            store(even)
-            store(odd)
+            for j, side in halves_for_vector(q):
+                if side is RIGHT:
+                    half = results[q][:, j % 2, RIGHT]
+                    nc.vector.tensor_tensor(out=half, in0=half, in1=m_right[:], op=ALU.mult)
+            for j in turned_tiles(q):
+                nc.vector.tensor_tensor(
+                    out=results[q][:, j % 2, RIGHT], in0=total[j][:], in1=m_all[:, RIGHT], op=ALU.mult
+                )
+            if last:
+                for j in (even, odd):
+                    for side in (RIGHT, LEFT):
+                        nc.sync.dma_start(out=out_rows[:, j, side], in_=results[q][:, j % 2, side])
+            else:
+                nc.sync.dma_start(out=out_rows[:, even : even + 2, :], in_=results[q][:])

@@ -315,15 +315,12 @@ def tile_loralinear_pa_t_kernel(tc, x, weight, a_w, b_w, magnitude, h_lora, out)
             rights = [(j, RIGHT) for j in (2 * q, 2 * q + 1) if j not in turned_tiles(q)]
             return rights + [(2 * q, LEFT), (2 * q + 1, LEFT)]
 
-        def adapters_of_pair(q):
-            for j, side in halves_for_vector(q):
-                adapter(j, side)
-
         def products_of_pair(q):
             for j, side in halves_for_vector(q):
                 product(j, side)
 
-        adapters_of_pair(0)
+        for j, side in halves_for_vector(0):
+            adapter(j, side)
         products_of_pair(0)
         transpose_token_pair(2, nc.vector.tensor_copy)
         m_left = psum.tile([P, BANK], F32, tag="ring", name="m_left")
@@ -342,11 +339,15 @@ def tile_loralinear_pa_t_kernel(tc, x, weight, a_w, b_w, magnitude, h_lora, out)
             for j in turned_tiles(q):
                 open_total(j)
             if q + 1 < PAIRS:
-                adapters_of_pair(q + 1)
+                *first_adapters, last_adapter = halves_for_vector(q + 1)
+                for j, side in first_adapters:
+                    adapter(j, side)
             for j in turned_tiles(q):
                 add_turned_product(j)
             if q + AHEAD < PAIRS:
                 transpose_token_pair(q + AHEAD, nc.scalar.copy)
+            if q + 1 < PAIRS:
+                adapter(*last_adapter)
             last = q == PAIRS - 1
             for j, side in halves_for_vector(q):
                 add(j, side)

@@ -299,9 +299,9 @@ def tile_loralinear_pa_t_kernel(tc, x, weight, a_w, b_w, magnitude, h_lora, out)
                 op=ALU.add,
             )
 
-        def scale_left(q, first, end):
+        def scale_left(engine, q, first, end):
             halves = results[q][:, first:end, LEFT]
-            nc.gpsimd.tensor_tensor(
+            engine.tensor_tensor(
                 out=halves,
                 in0=halves,
                 in1=m_all[:, LEFT].unsqueeze(1).to_broadcast([P, end - first, BANK]),
@@ -349,12 +349,13 @@ def tile_loralinear_pa_t_kernel(tc, x, weight, a_w, b_w, magnitude, h_lora, out)
             if q + 1 < PAIRS:
                 adapter(*last_adapter)
             last = q == PAIRS - 1
+            fine = q >= PAIRS - 2
             for j, side in halves_for_vector(q):
                 add(j, side)
-                if last:
-                    scale_left(q, j % 2, j % 2 + 1)
-            if not last:
-                scale_left(q, 0, 2)
+                if fine and not (last and j == odd):
+                    scale_left(nc.gpsimd, q, j % 2, j % 2 + 1)
+            if not fine:
+                scale_left(nc.gpsimd, q, 0, 2)
             if q + 2 < PAIRS:
                 quantise_token_pair(q + 2)
             for j, side in halves_for_vector(q):
@@ -366,8 +367,10 @@ def tile_loralinear_pa_t_kernel(tc, x, weight, a_w, b_w, magnitude, h_lora, out)
                     out=results[q][:, j % 2, RIGHT], in0=total[j][:], in1=m_all[:, RIGHT], op=ALU.mult
                 )
             if last:
-                for j in (even, odd):
-                    for side in (RIGHT, LEFT):
+                scale_left(nc.vector, q, 1, 2)
+            if fine:
+                for side in (RIGHT, LEFT):
+                    for j in (even, odd):
                         nc.sync.dma_start(out=out_rows[:, j, side], in_=results[q][:, j % 2, side])
             else:
                 nc.sync.dma_start(out=out_rows[:, even : even + 2, :], in_=results[q][:])

from contextlib import ExitStack

import concourse.mybir as mybir
from concourse.masks import make_identity

F32 = mybir.dt.float32
BF16 = mybir.dt.bfloat16
U32 = mybir.dt.uint32
U8 = mybir.dt.uint8
FP8X4 = mybir.dt.float8_e4m3fn_x4
ACT = mybir.ActivationFunctionType
ALU = mybir.AluOpType

P = 128
TOKENS = 4096
D_IN = 512
D_OUT = 1024
RANK = 128
BANK = 512
WORDS = D_IN // 2
TOKEN_TILES = TOKENS // P
OUT_TILES = D_OUT // P
LOAD_TILES = 4
PAIRS = TOKEN_TILES // 2
AHEAD = 3
WARM_UP = 4
SIDE_TILES = BANK // P

FLOPS = 2 * TOKENS * D_OUT * (D_IN + RANK) + 2 * D_OUT * RANK * D_IN


def tile_loralinear_pa_t_kernel(tc, x, weight, a_w, b_w, magnitude, h_lora, out):
    nc = tc.nc
    x_rows = x.flatten_outer_dims().rearrange("(p j) k -> p (j k)", j=TOKEN_TILES)
    h_rows = h_lora.flatten_outer_dims().rearrange("(p j) r -> p (j r)", j=TOKEN_TILES)
    out_rows = out.flatten_outer_dims().rearrange("(p j) o -> p j o", j=TOKEN_TILES)

    with ExitStack() as stack:
        keep = stack.enter_context(tc.tile_pool(name="keep", bufs=1))
        work = stack.enter_context(tc.tile_pool(name="work", bufs=2))
        psum = stack.enter_context(tc.psum_pool(name="psum", bufs=7))
        stack.enter_context(tc.manual_schedule())

        ident_bf16 = keep.tile([P, P], BF16, align_bytes=256)
        make_identity(nc, ident_bf16[:])
        ident_f32 = keep.tile([P, P], F32, align_bytes=256)
        make_identity(nc, ident_f32[:])
        one = keep.tile([P, 1], F32)
        nc.vector.memset(one[:], 1.0)
        nc.scalar.sqrt(one[:], one[:])

        zeros = keep.tile([P, BANK], BF16)
        nc.vector.memset(zeros[:], 0.0)
        warm = psum.tile([P, BANK], F32, tag="ring", name="warm")
        for i in range(WARM_UP):
            nc.tensor.matmul(warm[:], lhsT=zeros[:, 0:P], rhs=zeros[:], start=True, stop=True)

        w_sb = keep.tile([P, OUT_TILES * D_IN], BF16, align_bytes=256)
        x_sb = keep.tile([P, TOKEN_TILES * D_IN], BF16, align_bytes=256)
        h_sb = keep.tile([P, TOKEN_TILES * RANK], BF16, align_bytes=256)
        bw_sb = keep.tile([P, OUT_TILES * RANK], BF16, align_bytes=256)
        aw_sb = keep.tile([P, D_IN], BF16, align_bytes=256)
        mag_rows = keep.tile([P, P], BF16)
        nc.vector.memset(mag_rows[:], 0.0)

        def load_weight_half(half):
            tiles = OUT_TILES // 2
            nc.sync.dma_start(
                out=w_sb[:, half * tiles * D_IN : (half + 1) * tiles * D_IN].rearrange(
                    "p (a k) -> p a k", a=tiles
                ),
                in_=weight[half * tiles * P : (half + 1) * tiles * P, :].rearrange(
                    "(a p) k -> p a k", p=P
                ),
            )

        def load_x(c):
            cols = slice(c * LOAD_TILES * D_IN, (c + 1) * LOAD_TILES * D_IN)
            nc.sync.dma_start(out=x_sb[:, cols], in_=x_rows[:, cols])

        def load_h(c):
            cols = slice(c * 2 * LOAD_TILES * RANK, (c + 1) * 2 * LOAD_TILES * RANK)
            nc.sync.dma_start(out=h_sb[:, cols], in_=h_rows[:, cols])

        nc.sync.dma_start(
            out=bw_sb[:].rearrange("p (a r) -> p a r", a=OUT_TILES),
            in_=b_w.rearrange("(a p) r -> p a r", p=P),
        )
        nc.sync.dma_start(
            out=mag_rows[0:OUT_TILES, :], in_=magnitude.rearrange("u (a p) -> (u a) p", p=P)
        )
        load_weight_half(0)
        nc.sync.dma_start(out=aw_sb[:], in_=a_w)
        load_weight_half(1)
        for c in range(TOKEN_TILES // LOAD_TILES):
            load_x(c)
            if c % 2 == 0:
                load_h(c // 2)

        def regroup_two_row_tiles(words, first_tile, grouped_words, copy):
            bank = psum.tile([P, 2, 2, P], F32, tag="ring", name="bank")
            for i in range(2):
                for u in range(2):
                    first = (first_tile + i) * WORDS + u * P
                    nc.tensor.transpose(bank[:, i, u, :], words[:, first : first + P], ident_f32[:])
            copy(
                out=grouped_words.rearrange("p (i r u) -> p i r u", i=2, u=2),
                in_=bank[:].rearrange("p i u r -> p i r u"),
            )

        w_codes = keep.tile([P, D_OUT], U32, align_bytes=256)
        w_scales = keep.tile([P, D_OUT], U8, align_bytes=256)
        w_grouped = keep.tile([P, D_OUT * 4], BF16, align_bytes=256)
        x_codes = keep.tile([P, TOKENS], U32, align_bytes=256)
        x_scales = keep.tile([P, TOKENS], U8, align_bytes=256)
        hT = keep.tile([P, TOKENS], BF16, align_bytes=256)
        x_grouped = {}

        def transpose_token_pair(q, copy):
            x_grouped[q] = work.tile([P, 2 * P * 4], BF16, align_bytes=64, tag="xg", name="x_grouped", bufs=3)
            regroup_two_row_tiles(x_sb[:].bitcast(F32), 2 * q, x_grouped[q][:].bitcast(F32), copy)
            h_bank = psum.tile([P, 2 * P], BF16, tag="ring", name="h_bank")
            for i in range(2):
                j = 2 * q + i
                nc.tensor.transpose(
                    h_bank[:, i * P : (i + 1) * P], h_sb[:, j * RANK : (j + 1) * RANK], ident_bf16[:]
                )
            copy(out=hT[:, 2 * q * P : (2 * q + 2) * P], in_=h_bank[:])

        def quantise_token_pair(q):
            cols = slice(2 * q * P, (2 * q + 2) * P)
            nc.vector.quantize_mx(
                out=x_codes[:, cols].bitcast(FP8X4), scales=x_scales[:, cols], in_=x_grouped[q][:]
            )

        bwT2 = keep.tile([P, D_OUT], BF16, align_bytes=256)
        bw_banks = []
        for half in range(2):
            bw_bank = psum.tile([P, BANK], BF16, tag="ring", name="bw_bank")
            for i in range(SIDE_TILES):
                a = half * SIDE_TILES + i
                nc.tensor.transpose(
                    bw_bank[:, i * P : (i + 1) * P], bw_sb[:, a * RANK : (a + 1) * RANK], ident_bf16[:]
                )
            bw_banks.append(bw_bank)
        nc.scalar.mul(out=bwT2[:, 0:BANK], in_=bw_banks[0][:], mul=2.0)
        nc.vector.tensor_scalar(
            out=bwT2[:, BANK:D_OUT], in0=bw_banks[1][:], scalar1=2.0, scalar2=None, op0=ALU.mult
        )

        norm_sq = keep.tile([P, OUT_TILES], F32)

        def regroup_weight_pair(pair):
            regroup_two_row_tiles(
                w_sb[:].bitcast(F32),
                2 * pair,
                w_grouped[:].bitcast(F32)[:, pair * BANK : (pair + 1) * BANK],
                nc.vector.tensor_copy,
            )

        def quantise_weight_half(half):
            nc.vector.quantize_mx(
                out=w_codes[:, half * BANK : (half + 1) * BANK].bitcast(FP8X4),
                scales=w_scales[:, half * BANK : (half + 1) * BANK],
                in_=w_grouped[:, half * BANK * 4 : (half + 1) * BANK * 4],
            )

        def square_norms(a):
            w_eff = psum.tile([P, D_IN], F32, tag="ring", name="w_eff")
            nc.tensor.matmul(
                w_eff[:], lhsT=bwT2[:, a * P : (a + 1) * P], rhs=aw_sb[:], start=True, stop=False
            )
            nc.tensor.matmul(
                w_eff[:],
                lhsT=ident_bf16[:],
                rhs=w_sb[:, a * D_IN : (a + 1) * D_IN],
                start=False,
                stop=True,
            )
            squares = work.tile([P, D_IN], F32, tag="sq", name="squares")
            nc.scalar.activation(
                out=squares[:], in_=w_eff[:], func=ACT.Square, accum_out=norm_sq[:, a : a + 1]
            )

        regroup_weight_pair(0)
        square_norms(0)
        square_norms(1)
        regroup_weight_pair(1)
        square_norms(2)
        square_norms(3)
        regroup_weight_pair(2)
        quantise_weight_half(0)
        square_norms(4)
        square_norms(5)
        regroup_weight_pair(3)
        square_norms(6)
        transpose_token_pair(0, nc.vector.tensor_copy)
        square_norms(7)
        quantise_token_pair(0)
        quantise_weight_half(1)
        transpose_token_pair(1, nc.vector.tensor_copy)
        quantise_token_pair(1)
        mag_bank = psum.tile([P, P], BF16, tag="ring", name="mag_bank")
        nc.tensor.transpose(mag_bank[:], mag_rows[:], ident_bf16[:])
        mag_col = keep.tile([P, OUT_TILES], F32)
        nc.vector.tensor_copy(out=mag_col[:], in_=mag_bank[:, 0:OUT_TILES])

        norm = keep.tile([P, OUT_TILES], F32)
        nc.scalar.sqrt(norm[:], norm_sq[:])
        m_col = keep.tile([P, OUT_TILES], F32)
        nc.vector.reciprocal(m_col[:], norm[:])
        nc.vector.tensor_tensor(out=m_col[:], in0=m_col[:], in1=mag_col[:], op=ALU.mult)
        m_all = keep.tile([P, D_OUT], F32)
        m_right = psum.tile([P, BANK], F32, tag="m", bufs=1)

        def spread_m(half, m_bank):
            for i in range(SIDE_TILES):
                a = half * SIDE_TILES + i
                nc.tensor.transpose(
                    m_bank[:, i * P : (i + 1) * P],
                    m_col[:, a : a + 1].to_broadcast([P, P]),
                    ident_f32[:],
                )
            nc.scalar.copy(out=m_all[:, half * BANK : (half + 1) * BANK], in_=m_bank[:])

        LEFT = slice(0, BANK)
        RIGHT = slice(BANK, D_OUT)
        lora_sb = {}
        baseT_sb = {}
        base = {}
        total = {}
        results = {}

        def adapter(j, side):
            lora = psum.tile([P, BANK], F32, tag="ring", name="lora")
            nc.tensor.matmul(
                lora[:], lhsT=hT[:, j * P : (j + 1) * P], rhs=bwT2[:, side], start=True, stop=True
            )
            lora_sb[j, side.start] = work.tile([P, BANK], F32, tag="lsb", name="lora_sb", bufs=6)
            nc.scalar.copy(out=lora_sb[j, side.start][:], in_=lora[:])

        def product_turned(j):
            tokens = slice(j * P, (j + 1) * P)
            bank = psum.tile([P, SIDE_TILES * P], F32, tag="ring", name="baseT")
            for i in range(SIDE_TILES):
                a = SIDE_TILES + i
                nc.tensor.matmul_mx(
                    out=bank[:, i * P : (i + 1) * P],
                    lhsT=w_codes[:, a * P : (a + 1) * P].bitcast(FP8X4),
                    lhsT_scale=w_scales[:, a * P : (a + 1) * P],
                    rhs=x_codes[:, tokens].bitcast(FP8X4),
                    rhs_scale=x_scales[:, tokens],
                    start=True,
                    stop=True,
                )
            baseT_sb[j] = work.tile([P, SIDE_TILES * P], F32, tag="bT", name="baseT_sb", bufs=4, align_bytes=256)
            nc.scalar.copy(out=baseT_sb[j][:], in_=bank[:])

        def product(j, side):
            rows = slice(j * P, (j + 1) * P)
            base[j, side.start] = psum.tile([P, BANK], F32, tag="ring", name="base")
            nc.tensor.matmul_mx(
                out=base[j, side.start][:],
                lhsT=x_codes[:, rows].bitcast(FP8X4),
                lhsT_scale=x_scales[:, rows],
                rhs=w_codes[:, side].bitcast(FP8X4),
                rhs_scale=w_scales[:, side],
                start=True,
                stop=True,
            )

        def open_total(j):
            total[j] = psum.tile([P, BANK], F32, tag="ring", name="total")
            nc.tensor.matmul(
                total[j][:],
                lhsT=hT[:, j * P : (j + 1) * P],
                rhs=bwT2[:, RIGHT],
                start=True,
                stop=False,
            )

        def add_turned_product(j):
            for a in range(SIDE_TILES):
                nc.tensor.matmul(
                    total[j][:, a * P : (a + 1) * P],
                    lhsT=baseT_sb[j][:, a * P : (a + 1) * P],
                    rhs=ident_f32[:],
                    is_transpose=True,
                    start=False,
                    stop=a == SIDE_TILES - 1,
                )

        def add(j, side):
            q, i = divmod(j, 2)
            nc.vector.tensor_tensor(
                out=results[q][:, i, side],
                in0=base[j, side.start][:],
                in1=lora_sb[j, side.start][:],
                op=ALU.add,
            )

        def scale_left(engine, q, first, end):
            halves = results[q][:, first:end, LEFT]
            engine.tensor_tensor(
                out=halves,
                in0=halves,
                in1=m_all[:, LEFT].unsqueeze(1).to_broadcast([P, end - first, BANK]),
                op=ALU.mult,
            )

        def turned_tiles(q):
            return (2 * q, 2 * q + 1) if q >= PAIRS - 2 else (2 * q,)

        def halves_for_vector(q):
            rights = [(j, RIGHT) for j in (2 * q, 2 * q + 1) if j not in turned_tiles(q)]
            return rights + [(2 * q, LEFT), (2 * q + 1, LEFT)]

        def products_of_pair(q):
            for j, side in halves_for_vector(q):
                product(j, side)

        for j, side in halves_for_vector(0):
            adapter(j, side)
        products_of_pair(0)
        transpose_token_pair(2, nc.vector.tensor_copy)
        m_left = psum.tile([P, BANK], F32, tag="ring", name="m_left")
        spread_m(0, m_left)
        for j in turned_tiles(0):
            product_turned(j)
        spread_m(1, m_right)
        for q in range(PAIRS):
            even, odd = 2 * q, 2 * q + 1
            results[q] = work.tile([P, 2, D_OUT], F32, tag="res", name="result", bufs=4)
            if q + 1 < PAIRS:
                for j in turned_tiles(q + 1):
                    product_turned(j)
            if q > 0:
                products_of_pair(q)
            for j in turned_tiles(q):
                open_total(j)
            if q + 1 < PAIRS:
                *first_adapters, last_adapter = halves_for_vector(q + 1)
                for j, side in first_adapters:
                    adapter(j, side)
            for j in turned_tiles(q):
                add_turned_product(j)
            if q + AHEAD < PAIRS:
                transpose_token_pair(q + AHEAD, nc.scalar.copy)
            if q + 1 < PAIRS:
                adapter(*last_adapter)
            last = q == PAIRS - 1
            fine = q >= PAIRS - 2
            for j, side in halves_for_vector(q):
                add(j, side)
                if fine and not (last and j == odd):
                    scale_left(nc.gpsimd, q, j % 2, j % 2 + 1)
            if not fine:
                scale_left(nc.gpsimd, q, 0, 2)
            if q + 2 < PAIRS:
                quantise_token_pair(q + 2)
            for j, side in halves_for_vector(q):
                if side is RIGHT:
                    half = results[q][:, j % 2, RIGHT]
                    nc.vector.tensor_tensor(out=half, in0=half, in1=m_right[:], op=ALU.mult)
            for j in turned_tiles(q):
                nc.vector.tensor_tensor(
                    out=results[q][:, j % 2, RIGHT], in0=total[j][:], in1=m_all[:, RIGHT], op=ALU.mult
                )
            if last:
                scale_left(nc.vector, q, 1, 2)
            if fine:
                for side in (RIGHT, LEFT):
                    for j in (even, odd):
                        nc.sync.dma_start(out=out_rows[:, j, side], in_=results[q][:, j % 2, side])
            else:
                nc.sync.dma_start(out=out_rows[:, even : even + 2, :], in_=results[q][:])
